import numpy as np
import ml_dtypes


def mxq(x, axis, fmt="e4m3"):
    dtype, down = {"e4m3": (ml_dtypes.float8_e4m3fn, 7), "e5m2": (ml_dtypes.float8_e5m2, 14)}[fmt]
    v = np.moveaxis(np.asarray(x, np.float32).astype(ml_dtypes.bfloat16).astype(np.float64), axis, -1)
    blocks = v.reshape(v.shape[:-1] + (-1, 32))
    amax = np.abs(blocks).max(-1, keepdims=True)
    byte = np.maximum(np.where(amax > 0, np.frexp(amax)[1] - 1 + 127, 0) - down, 1)
    scale = np.exp2(byte - 127.0)
    codes = (blocks / scale).astype(np.float32).astype(dtype).astype(np.float64)
    return np.moveaxis((codes * scale).reshape(v.shape), -1, axis)


WIDE = False


def mx_kscale(k):
    if not WIDE:
        return np.ones(k)
    levels = np.array([10, -10, 5, -5, 0])
    a = np.random.permutation(np.resize(levels, k // 512 * 4)).reshape(k // 512, 4)
    idx = np.arange(k)
    return np.exp2(a[idx // 512, idx % 128 // 32])


BF16 = ml_dtypes.bfloat16


def bf(x):
    return np.asarray(x, np.float32).astype(BF16)


def f64(x):
    return np.asarray(x).astype(np.float64)


B, N, D, R = 8, 1024, 512, 4
M = N // R


def merge(t, r):
    b, n, d = t.shape
    return t.reshape(b, n // r, r, d).mean(axis=2)


def setup_inputs():
    s, t = mx_kscale(D), mx_kscale(D)
    a = 2.0 / np.sqrt(D)
    return {"x": bf(np.random.standard_normal((B, N, D)) * s),
            "Wq": bf(np.random.standard_normal((D, D)) * a * t[:, None] / s),
            "bq": bf(np.random.standard_normal(D) * 0.5 * t),
            "Wk": bf(np.random.standard_normal((D, D)) * a / t[:, None] / s),
            "bk": bf(np.random.standard_normal(D) * 0.3 / t)}


def reference(x, Wq, bq, Wk, bk):
    xq = mxq(f64(x), 2, "e4m3")
    Q = (xq @ mxq(f64(Wq), 1, "e4m3").T) + f64(bq)
    K = (xq @ mxq(f64(Wk), 1, "e4m3").T) + f64(bk)
    K_m = merge(K, R)
    scores = (mxq(Q, 2, "e4m3") @ mxq(K_m, 2, "e4m3").transpose(0, 2, 1)) * (1.0 / np.sqrt(D))
    return scores + np.log(R)

@@ -1,0 +1,213 @@
+import math
+from contextlib import ExitStack
+
+import concourse.mybir as mybir
+from concourse.masks import make_identity
+
+F32 = mybir.dt.float32
+BF16 = mybir.dt.bfloat16
+U32 = mybir.dt.uint32
+U8 = mybir.dt.uint8
+FP8X4 = mybir.dt.float8_e4m3fn_x4
+ADD = mybir.AluOpType.add
+MULT = mybir.AluOpType.mult
+IDENTITY = mybir.ActivationFunctionType.Identity
+COPY = mybir.ActivationFunctionType.Copy
+
+P = 128
+PACK = 4
+D = P * PACK
+BATCH = 8
+TOKENS = 1024
+WINDOW = 4
+KEYS = TOKENS // WINDOW
+BLOCK = P * WINDOW
+BLOCKS = BATCH * TOKENS // BLOCK
+BLOCKS_PER_BATCH = TOKENS // BLOCK
+PAIR = 2 * P
+SCORE_LAG = 3
+
+FLOPS = 2 * BATCH * TOKENS * D * D * 2 + 2 * BATCH * TOKENS * KEYS * D
+
+
+def tile_siglipsdpaattention_pa_t_kernel(tc, x, Wq, bq, Wk, bk, out):
+    nc = tc.nc
+    x_rows = x.flatten_outer_dims()
+    out_rows = out.flatten_outer_dims()
+
+    with ExitStack() as ctx:
+        ctx.enter_context(tc.manual_schedule())
+        const = ctx.enter_context(tc.tile_pool(name="const", bufs=1))
+        x_pool = ctx.enter_context(tc.tile_pool(name="x_pool", bufs=BLOCKS))
+        work = ctx.enter_context(tc.tile_pool(name="work", bufs=2))
+        x_mx = ctx.enter_context(tc.tile_pool(name="x_mx", bufs=3))
+        q_mx = ctx.enter_context(tc.tile_pool(name="q_mx", bufs=SCORE_LAG + 2))
+        k_mx = ctx.enter_context(tc.tile_pool(name="k_mx", bufs=3))
+        out_pool = ctx.enter_context(tc.tile_pool(name="out_pool", bufs=4))
+        flip_psum = ctx.enter_context(tc.psum_pool(name="flip_psum", bufs=2))
+        qv_psum = ctx.enter_context(tc.psum_pool(name="qv_psum", bufs=2))
+        qs_psum = ctx.enter_context(tc.psum_pool(name="qs_psum", bufs=2))
+        k_psum = ctx.enter_context(tc.psum_pool(name="k_psum", bufs=1))
+        score_psum = ctx.enter_context(tc.psum_pool(name="score_psum", bufs=1))
+
+        def load_four_rows_a_partition(rows, tile_sb):
+            nc.sync.dma_start(out=tile_sb[:], in_=rows.rearrange("(p s) d -> p (s d)", s=PACK))
+
+        wq_sb = const.tile([P, PACK * D], BF16)
+        wk_sb = const.tile([P, PACK * D], BF16)
+        load_four_rows_a_partition(Wq, wq_sb)
+        load_four_rows_a_partition(Wk, wk_sb)
+        x_sb = []
+        for n in range(BLOCKS):
+            x_block = x_pool.tile([P, PACK * D], BF16, name="x_block")
+            load_four_rows_a_partition(x_rows[n * BLOCK : (n + 1) * BLOCK, :], x_block)
+            x_sb.append(x_block)
+
+        bq_bf = const.tile([P, PACK], BF16)
+        bk_bf = const.tile([P, PACK], BF16)
+        nc.scalar.dma_start(out=bq_bf[:], in_=bq.rearrange("(p j) -> p j", j=PACK))
+        nc.scalar.dma_start(out=bk_bf[:], in_=bk.rearrange("(p j) -> p j", j=PACK))
+
+        ident = const.tile([P, P], F32)
+        make_identity(nc, ident[:])
+
+        def features_to_partitions(rows_sb, grouped, copy_out):
+            words = rows_sb[:].bitcast(F32)
+            grouped_words = grouped[:].bitcast(F32).rearrange("p (c u) -> p c u", u=2)
+            for half in range(2):
+                flipped = flip_psum.tile([P, 2, PAIR], F32, name="flipped")
+                for s in range(2):
+                    for u in range(2):
+                        first = (2 * half + s) * (D // 2) + u * P
+                        nc.tensor.transpose(
+                            flipped[:, u, s * P : (s + 1) * P], words[:, first : first + P], ident[:]
+                        )
+                copy_out(
+                    out=grouped_words[:, half * PAIR : (half + 1) * PAIR, :],
+                    in_=flipped[:].rearrange("p u c -> p c u"),
+                )
+
+        def quantise(grouped_flat, codes, scales):
+            nc.vector.quantize_mx(out=codes.bitcast(FP8X4), scales=scales, in_=grouped_flat)
+
+        def mx_pass(acc, lhs, lhs_cols, rhs, rhs_cols, start, stop):
+            nc.tensor.matmul_mx(
+                out=acc,
+                lhsT=lhs[0][:, lhs_cols].bitcast(FP8X4),
+                lhsT_scale=lhs[1][:, lhs_cols],
+                rhs=rhs[0][:, rhs_cols].bitcast(FP8X4),
+                rhs_scale=rhs[1][:, rhs_cols],
+                start=start,
+                stop=stop,
+            )
+
+        def set_of(i):
+            return slice(i * P, (i + 1) * P)
+
+        weights = []
+        for label, w_sb in (("wq", wq_sb), ("wk", wk_sb)):
+            w_grouped = const.tile([P, PACK * D], BF16, name="%s_grouped" % label, align_bytes=64)
+            w_codes = const.tile([P, D], U32, name="%s_codes" % label, align_bytes=64)
+            w_scales = const.tile([P, D], U8, name="%s_scales" % label, align_bytes=64)
+            features_to_partitions(w_sb, w_grouped, nc.vector.tensor_copy)
+            weights.append((w_grouped, w_codes, w_scales))
+        for w_grouped, w_codes, w_scales in weights:
+            quantise(w_grouped[:], w_codes[:], w_scales[:])
+        wq_mx = (weights[0][1], weights[0][2])
+        wk_mx = (weights[1][1], weights[1][2])
+
+        bq_f32 = const.tile([P, PACK], F32)
+        bk_f32 = const.tile([P, PACK], F32)
+        nc.vector.tensor_copy(out=bq_f32[:], in_=bq_bf[:])
+        nc.vector.tensor_copy(out=bk_f32[:], in_=bk_bf[:])
+        bq_every_column = bq_f32[:].unsqueeze(1).to_broadcast([P, P, PACK])
+        bk_every_column = bk_f32[:].unsqueeze(1).to_broadcast([P, P, PACK])
+
+        x_codes = {}
+        q_codes = {}
+        k_codes = {}
+
+        def prepare_x(n):
+            x_grouped = work.tile([P, PACK * BLOCK], BF16, name="x_grouped", align_bytes=64)
+            features_to_partitions(x_sb[n], x_grouped, nc.scalar.copy)
+            codes = x_mx.tile([P, BLOCK], U32, name="x_code_words", align_bytes=64)
+            scales = x_mx.tile([P, BLOCK], U8, name="x_scale_bytes", align_bytes=64)
+            quantise(x_grouped[:], codes[:], scales[:])
+            x_codes[n] = (codes, scales)
+
+        def scores(n, pair):
+            acc = score_psum.tile([P, 2, KEYS], F32, name="score_acc")
+            for i in range(2):
+                mx_pass(
+                    acc[:, i, :], q_codes[n], set_of(2 * pair + i),
+                    k_codes[n // BLOCKS_PER_BATCH], slice(0, KEYS), True, True,
+                )
+            logits = out_pool.tile([P, 2, KEYS], F32, name="logits")
+            nc.scalar.activation(
+                out=logits[:], in_=acc[:], func=COPY, bias=math.log(WINDOW), scale=1.0 / math.sqrt(D)
+            )
+            block_rows = out_rows[n * BLOCK : (n + 1) * BLOCK, :].rearrange("(m r) k -> m r k", r=WINDOW)
+            nc.sync.dma_start(out=block_rows[:, 2 * pair : 2 * pair + 2, :], in_=logits[:])
+
+        prepare_x(0)
+        for n in range(BLOCKS + SCORE_LAG):
+            if n + 1 < BLOCKS:
+                prepare_x(n + 1)
+            if n >= SCORE_LAG:
+                scores(n - SCORE_LAG, 0)
+
+            if n < BLOCKS:
+                q_grouped = work.tile([P, BLOCK, PACK], BF16, name="q_grouped", align_bytes=64)
+
+                q_planes = work.tile([P, PACK, PAIR], BF16, name="q_planes")
+                for jj in range(2):
+                    qs_acc = qs_psum.tile([P, 2, PAIR], F32, name="qs_acc")
+                    for i in range(2):
+                        mx_pass(qs_acc[:, i, :], wq_mx, set_of(2 * jj + i), x_codes[n], slice(PAIR, 2 * PAIR), True, True)
+                    for i in range(2):
+                        j = 2 * jj + i
+                        nc.scalar.activation(
+                            out=q_planes[:, j, :], in_=qs_acc[:, i, :], func=IDENTITY,
+                            bias=bq_f32[:, j : j + 1], scale=1.0,
+                        )
+
+                k_acc = k_psum.tile([P, PACK, P], F32, name="k_acc")
+                for j in range(PACK):
+                    for r in range(WINDOW):
+                        mx_pass(k_acc[:, j, :], wk_mx, set_of(j), x_codes[n], set_of(r), r == 0, r == WINDOW - 1)
+                k_grouped = work.tile([P, P, PACK], BF16, name="k_grouped", align_bytes=64)
+                nc.vector.scalar_tensor_tensor(
+                    out=k_grouped[:], in0=k_acc[:].rearrange("p j m -> p m j"), scalar=1.0 / WINDOW,
+                    in1=bk_every_column, op0=MULT, op1=ADD,
+                )
+
+            if n >= SCORE_LAG:
+                scores(n - SCORE_LAG, 1)
+
+            if n < BLOCKS:
+                for r in range(2):
+                    qv_acc = qv_psum.tile([P, PACK, P], F32, name="qv_acc")
+                    for j in range(PACK):
+                        mx_pass(qv_acc[:, j, :], wq_mx, set_of(j), x_codes[n], set_of(r), True, True)
+                    nc.vector.tensor_tensor(
+                        out=q_grouped[:, set_of(r), :], in0=qv_acc[:].rearrange("p j m -> p m j"),
+                        in1=bq_every_column, op=ADD,
+                    )
+                    if r == 0:
+                        nc.vector.tensor_copy(
+                            out=q_grouped[:, PAIR : 2 * PAIR, :].rearrange("p (c i) j -> p c j i", i=4),
+                            in_=q_planes[:].rearrange("p j (c i) -> p c j i", i=4),
+                        )
+
+                half = n % BLOCKS_PER_BATCH
+                if half == 0:
+                    k_words = k_mx.tile([P, KEYS], U32, name="k_words", align_bytes=64)
+                    k_bytes = k_mx.tile([P, KEYS], U8, name="k_bytes", align_bytes=64)
+                    k_codes[n // BLOCKS_PER_BATCH] = (k_words, k_bytes)
+                k_words, k_bytes = k_codes[n // BLOCKS_PER_BATCH]
+                quantise(k_grouped[:].rearrange("p m j -> p (m j)"), k_words[:, set_of(half)], k_bytes[:, set_of(half)])
+
+                q_words = q_mx.tile([P, BLOCK], U32, name="q_words", align_bytes=64)
+                q_bytes = q_mx.tile([P, BLOCK], U8, name="q_bytes", align_bytes=64)
+                quantise(q_grouped[:].rearrange("p c j -> p (c j)"), q_words[:], q_bytes[:])
+                q_codes[n] = (q_words, q_bytes)

@@ -25,6 +25,7 @@ BLOCK = P * WINDOW
 BLOCKS = BATCH * TOKENS // BLOCK
 BLOCKS_PER_BATCH = TOKENS // BLOCK
 PAIR = 2 * P
+PSUM_BANKS = 8
 SCORE_LAG = 3
 
 FLOPS = 2 * BATCH * TOKENS * D * D * 2 + 2 * BATCH * TOKENS * KEYS * D
@@ -44,11 +45,7 @@ def tile_siglipsdpaattention_pa_t_kernel(tc, x, Wq, bq, Wk, bk, out):
         q_mx = ctx.enter_context(tc.tile_pool(name="q_mx", bufs=SCORE_LAG + 2))
         k_mx = ctx.enter_context(tc.tile_pool(name="k_mx", bufs=3))
         out_pool = ctx.enter_context(tc.tile_pool(name="out_pool", bufs=4))
-        flip_psum = ctx.enter_context(tc.psum_pool(name="flip_psum", bufs=2))
-        qv_psum = ctx.enter_context(tc.psum_pool(name="qv_psum", bufs=2))
-        qs_psum = ctx.enter_context(tc.psum_pool(name="qs_psum", bufs=2))
-        k_psum = ctx.enter_context(tc.psum_pool(name="k_psum", bufs=1))
-        score_psum = ctx.enter_context(tc.psum_pool(name="score_psum", bufs=1))
+        psum = ctx.enter_context(tc.psum_pool(name="psum", bufs=PSUM_BANKS))
 
         def load_four_rows_a_partition(rows, tile_sb):
             nc.sync.dma_start(out=tile_sb[:], in_=rows.rearrange("(p s) d -> p (s d)", s=PACK))
@@ -75,7 +72,7 @@ def tile_siglipsdpaattention_pa_t_kernel(tc, x, Wq, bq, Wk, bk, out):
             words = rows_sb[:].bitcast(F32)
             grouped_words = grouped[:].bitcast(F32).rearrange("p (c u) -> p c u", u=2)
             for half in range(2):
-                flipped = flip_psum.tile([P, 2, PAIR], F32, name="flipped")
+                flipped = psum.tile([P, 2, PAIR], F32, name="flipped", tag="bank")
                 for s in range(2):
                     for u in range(2):
                         first = (2 * half + s) * (D // 2) + u * P
@@ -136,7 +133,7 @@ def tile_siglipsdpaattention_pa_t_kernel(tc, x, Wq, bq, Wk, bk, out):
             x_codes[n] = (codes, scales)
 
         def scores(n, pair):
-            acc = score_psum.tile([P, 2, KEYS], F32, name="score_acc")
+            acc = psum.tile([P, 2, KEYS], F32, name="score_acc", tag="bank")
             for i in range(2):
                 mx_pass(
                     acc[:, i, :], q_codes[n], set_of(2 * pair + i),
@@ -161,7 +158,7 @@ def tile_siglipsdpaattention_pa_t_kernel(tc, x, Wq, bq, Wk, bk, out):
 
                 q_planes = work.tile([P, PACK, PAIR], BF16, name="q_planes")
                 for jj in range(2):
-                    qs_acc = qs_psum.tile([P, 2, PAIR], F32, name="qs_acc")
+                    qs_acc = psum.tile([P, 2, PAIR], F32, name="qs_acc", tag="bank")
                     for i in range(2):
                         mx_pass(qs_acc[:, i, :], wq_mx, set_of(2 * jj + i), x_codes[n], slice(PAIR, 2 * PAIR), True, True)
                     for i in range(2):
@@ -171,7 +168,7 @@ def tile_siglipsdpaattention_pa_t_kernel(tc, x, Wq, bq, Wk, bk, out):
                             bias=bq_f32[:, j : j + 1], scale=1.0,
                         )
 
-                k_acc = k_psum.tile([P, PACK, P], F32, name="k_acc")
+                k_acc = psum.tile([P, PACK, P], F32, name="k_acc", tag="bank")
                 for j in range(PACK):
                     for r in range(WINDOW):
                         mx_pass(k_acc[:, j, :], wk_mx, set_of(j), x_codes[n], set_of(r), r == 0, r == WINDOW - 1)
@@ -186,7 +183,7 @@ def tile_siglipsdpaattention_pa_t_kernel(tc, x, Wq, bq, Wk, bk, out):
 
             if n < BLOCKS:
                 for r in range(2):
-                    qv_acc = qv_psum.tile([P, PACK, P], F32, name="qv_acc")
+                    qv_acc = psum.tile([P, PACK, P], F32, name="qv_acc", tag="bank")
                     for j in range(PACK):
                         mx_pass(qv_acc[:, j, :], wq_mx, set_of(j), x_codes[n], set_of(r), True, True)
                     nc.vector.tensor_tensor(

@@ -41,6 +41,7 @@ def tile_siglipsdpaattention_pa_t_kernel(tc, x, Wq, bq, Wk, bk, out):
         const = ctx.enter_context(tc.tile_pool(name="const", bufs=1))
         x_pool = ctx.enter_context(tc.tile_pool(name="x_pool", bufs=BLOCKS))
         work = ctx.enter_context(tc.tile_pool(name="work", bufs=2))
+        q_pool = ctx.enter_context(tc.tile_pool(name="q_pool", bufs=3))
         x_mx = ctx.enter_context(tc.tile_pool(name="x_mx", bufs=3))
         q_mx = ctx.enter_context(tc.tile_pool(name="q_mx", bufs=SCORE_LAG + 2))
         k_mx = ctx.enter_context(tc.tile_pool(name="k_mx", bufs=3))
@@ -146,65 +147,80 @@ def tile_siglipsdpaattention_pa_t_kernel(tc, x, Wq, bq, Wk, bk, out):
             block_rows = out_rows[n * BLOCK : (n + 1) * BLOCK, :].rearrange("(m r) k -> m r k", r=WINDOW)
             nc.sync.dma_start(out=block_rows[:, 2 * pair : 2 * pair + 2, :], in_=logits[:])
 
+        q_grouped = {}
+
+        def q_for_scalar(n):
+            q_grouped[n] = q_pool.tile([P, BLOCK, PACK], BF16, name="q_grouped", align_bytes=64)
+            q_planes = work.tile([P, PACK, PAIR], BF16, name="q_planes")
+            for jj in range(2):
+                qs_acc = psum.tile([P, 2, PAIR], F32, name="qs_acc", tag="bank")
+                for i in range(2):
+                    mx_pass(qs_acc[:, i, :], wq_mx, set_of(2 * jj + i), x_codes[n], slice(PAIR, 2 * PAIR), True, True)
+                for i in range(2):
+                    j = 2 * jj + i
+                    nc.scalar.activation(
+                        out=q_planes[:, j, :], in_=qs_acc[:, i, :], func=IDENTITY,
+                        bias=bq_f32[:, j : j + 1], scale=1.0,
+                    )
+            nc.gpsimd.tensor_scalar(
+                out=q_grouped[n][:, PAIR : 2 * PAIR, :], in0=q_planes[:].rearrange("p j c -> p c j"),
+                scalar1=1.0, scalar2=0.0, op0=MULT, op1=ADD,
+            )
+
+        def q_for_vector(n):
+            for r in range(2):
+                qv_acc = psum.tile([P, PACK, P], F32, name="qv_acc", tag="bank")
+                for j in range(PACK):
+                    mx_pass(qv_acc[:, j, :], wq_mx, set_of(j), x_codes[n], set_of(r), True, True)
+                nc.vector.tensor_tensor(
+                    out=q_grouped[n][:, set_of(r), :], in0=qv_acc[:].rearrange("p j c -> p c j"),
+                    in1=bq_every_column, op=ADD,
+                )
+
+        def quantise_q(n):
+            q_words = q_mx.tile([P, BLOCK], U32, name="q_words", align_bytes=64)
+            q_bytes = q_mx.tile([P, BLOCK], U8, name="q_bytes", align_bytes=64)
+            quantise(q_grouped[n][:].rearrange("p c j -> p (c j)"), q_words[:], q_bytes[:])
+            q_codes[n] = (q_words, q_bytes)
+
+        k_grouped = {}
+
+        def merged_k(n):
+            k_acc = psum.tile([P, PACK, P], F32, name="k_acc", tag="bank")
+            for j in range(PACK):
+                for r in range(WINDOW):
+                    mx_pass(k_acc[:, j, :], wk_mx, set_of(j), x_codes[n], set_of(r), r == 0, r == WINDOW - 1)
+            k_grouped[n] = work.tile([P, P, PACK], BF16, name="k_grouped", align_bytes=64)
+            nc.vector.scalar_tensor_tensor(
+                out=k_grouped[n][:], in0=k_acc[:].rearrange("p j m -> p m j"), scalar=1.0 / WINDOW,
+                in1=bk_every_column, op0=MULT, op1=ADD,
+            )
+
+        def quantise_k(n):
+            b = n // BLOCKS_PER_BATCH
+            half = n % BLOCKS_PER_BATCH
+            if half == 0:
+                k_words = k_mx.tile([P, KEYS], U32, name="k_words", align_bytes=64)
+                k_bytes = k_mx.tile([P, KEYS], U8, name="k_bytes", align_bytes=64)
+                k_codes[b] = (k_words, k_bytes)
+            quantise(
+                k_grouped[n][:].rearrange("p m j -> p (m j)"),
+                k_codes[b][0][:, set_of(half)], k_codes[b][1][:, set_of(half)],
+            )
+
         prepare_x(0)
         for n in range(BLOCKS + SCORE_LAG):
             if n + 1 < BLOCKS:
                 prepare_x(n + 1)
+            if 1 <= n <= BLOCKS:
+                quantise_q(n - 1)
             if n >= SCORE_LAG:
                 scores(n - SCORE_LAG, 0)
-
             if n < BLOCKS:
-                q_grouped = work.tile([P, BLOCK, PACK], BF16, name="q_grouped", align_bytes=64)
-
-                q_planes = work.tile([P, PACK, PAIR], BF16, name="q_planes")
-                for jj in range(2):
-                    qs_acc = psum.tile([P, 2, PAIR], F32, name="qs_acc", tag="bank")
-                    for i in range(2):
-                        mx_pass(qs_acc[:, i, :], wq_mx, set_of(2 * jj + i), x_codes[n], slice(PAIR, 2 * PAIR), True, True)
-                    for i in range(2):
-                        j = 2 * jj + i
-                        nc.scalar.activation(
-                            out=q_planes[:, j, :], in_=qs_acc[:, i, :], func=IDENTITY,
-                            bias=bq_f32[:, j : j + 1], scale=1.0,
-                        )
-
-                k_acc = psum.tile([P, PACK, P], F32, name="k_acc", tag="bank")
-                for j in range(PACK):
-                    for r in range(WINDOW):
-                        mx_pass(k_acc[:, j, :], wk_mx, set_of(j), x_codes[n], set_of(r), r == 0, r == WINDOW - 1)
-                k_grouped = work.tile([P, P, PACK], BF16, name="k_grouped", align_bytes=64)
-                nc.vector.scalar_tensor_tensor(
-                    out=k_grouped[:], in0=k_acc[:].rearrange("p j m -> p m j"), scalar=1.0 / WINDOW,
-                    in1=bk_every_column, op0=MULT, op1=ADD,
-                )
-
+                q_for_scalar(n)
+                merged_k(n)
             if n >= SCORE_LAG:
                 scores(n - SCORE_LAG, 1)
-
             if n < BLOCKS:
-                for r in range(2):
-                    qv_acc = psum.tile([P, PACK, P], F32, name="qv_acc", tag="bank")
-                    for j in range(PACK):
-                        mx_pass(qv_acc[:, j, :], wq_mx, set_of(j), x_codes[n], set_of(r), True, True)
-                    nc.vector.tensor_tensor(
-                        out=q_grouped[:, set_of(r), :], in0=qv_acc[:].rearrange("p j m -> p m j"),
-                        in1=bq_every_column, op=ADD,
-                    )
-                    if r == 0:
-                        nc.vector.tensor_copy(
-                            out=q_grouped[:, PAIR : 2 * PAIR, :].rearrange("p (c i) j -> p c j i", i=4),
-                            in_=q_planes[:].rearrange("p j (c i) -> p c j i", i=4),
-                        )
-
-                half = n % BLOCKS_PER_BATCH
-                if half == 0:
-                    k_words = k_mx.tile([P, KEYS], U32, name="k_words", align_bytes=64)
-                    k_bytes = k_mx.tile([P, KEYS], U8, name="k_bytes", align_bytes=64)
-                    k_codes[n // BLOCKS_PER_BATCH] = (k_words, k_bytes)
-                k_words, k_bytes = k_codes[n // BLOCKS_PER_BATCH]
-                quantise(k_grouped[:].rearrange("p m j -> p (m j)"), k_words[:, set_of(half)], k_bytes[:, set_of(half)])
-
-                q_words = q_mx.tile([P, BLOCK], U32, name="q_words", align_bytes=64)
-                q_bytes = q_mx.tile([P, BLOCK], U8, name="q_bytes", align_bytes=64)
-                quantise(q_grouped[:].rearrange("p c j -> p (c j)"), q_words[:], q_bytes[:])
-                q_codes[n] = (q_words, q_bytes)
+                q_for_vector(n)
+                quantise_k(n)

@@ -26,6 +26,7 @@ BLOCKS = BATCH * TOKENS // BLOCK
 BLOCKS_PER_BATCH = TOKENS // BLOCK
 PAIR = 2 * P
 PSUM_BANKS = 8
+FLIP_RUN = 2
 SCORE_LAG = 3
 
 FLOPS = 2 * BATCH * TOKENS * D * D * 2 + 2 * BATCH * TOKENS * KEYS * D
@@ -41,6 +42,7 @@ def tile_siglipsdpaattention_pa_t_kernel(tc, x, Wq, bq, Wk, bk, out):
         const = ctx.enter_context(tc.tile_pool(name="const", bufs=1))
         x_pool = ctx.enter_context(tc.tile_pool(name="x_pool", bufs=BLOCKS))
         work = ctx.enter_context(tc.tile_pool(name="work", bufs=2))
+        flip_pool = ctx.enter_context(tc.tile_pool(name="flip_pool", bufs=FLIP_RUN + 1))
         q_pool = ctx.enter_context(tc.tile_pool(name="q_pool", bufs=3))
         x_mx = ctx.enter_context(tc.tile_pool(name="x_mx", bufs=3))
         q_mx = ctx.enter_context(tc.tile_pool(name="q_mx", bufs=SCORE_LAG + 2))
@@ -125,12 +127,16 @@ def tile_siglipsdpaattention_pa_t_kernel(tc, x, Wq, bq, Wk, bk, out):
         q_codes = {}
         k_codes = {}
 
-        def prepare_x(n):
-            x_grouped = work.tile([P, PACK * BLOCK], BF16, name="x_grouped", align_bytes=64)
-            features_to_partitions(x_sb[n], x_grouped, nc.scalar.copy)
+        x_grouped = {}
+
+        def flip_x(n):
+            x_grouped[n] = flip_pool.tile([P, PACK * BLOCK], BF16, name="x_grouped", align_bytes=64)
+            features_to_partitions(x_sb[n], x_grouped[n], nc.scalar.copy)
+
+        def quantise_x(n):
             codes = x_mx.tile([P, BLOCK], U32, name="x_code_words", align_bytes=64)
             scales = x_mx.tile([P, BLOCK], U8, name="x_scale_bytes", align_bytes=64)
-            quantise(x_grouped[:], codes[:], scales[:])
+            quantise(x_grouped[n][:], codes[:], scales[:])
             x_codes[n] = (codes, scales)
 
         def scores(n, pair):
@@ -208,10 +214,15 @@ def tile_siglipsdpaattention_pa_t_kernel(tc, x, Wq, bq, Wk, bk, out):
                 k_codes[b][0][:, set_of(half)], k_codes[b][1][:, set_of(half)],
             )
 
-        prepare_x(0)
+        for m in range(FLIP_RUN):
+            flip_x(m)
+        quantise_x(0)
         for n in range(BLOCKS + SCORE_LAG):
+            if (n + 1) % FLIP_RUN == 0:
+                for m in range(n + 1, min(n + 1 + FLIP_RUN, BLOCKS)):
+                    flip_x(m)
             if n + 1 < BLOCKS:
-                prepare_x(n + 1)
+                quantise_x(n + 1)
             if 1 <= n <= BLOCKS:
                 quantise_q(n - 1)
             if n >= SCORE_LAG:

@@ -21,13 +21,14 @@ BATCH = 8
 TOKENS = 1024
 WINDOW = 4
 KEYS = TOKENS // WINDOW
-BLOCK = P * WINDOW
+SET = 128
+BLOCK = SET * WINDOW
 BLOCKS = BATCH * TOKENS // BLOCK
 BLOCKS_PER_BATCH = TOKENS // BLOCK
-PAIR = 2 * P
 PSUM_BANKS = 8
-FLIP_RUN = 2
-SCORE_LAG = 3
+PER_BANK = 2
+HALVES = 2
+SCORE_LAG = 2
 
 FLOPS = 2 * BATCH * TOKENS * D * D * 2 + 2 * BATCH * TOKENS * KEYS * D
 
@@ -39,19 +40,43 @@ def tile_siglipsdpaattention_pa_t_kernel(tc, x, Wq, bq, Wk, bk, out):
 
     with ExitStack() as ctx:
         ctx.enter_context(tc.manual_schedule())
+
         const = ctx.enter_context(tc.tile_pool(name="const", bufs=1))
         x_pool = ctx.enter_context(tc.tile_pool(name="x_pool", bufs=BLOCKS))
-        work = ctx.enter_context(tc.tile_pool(name="work", bufs=2))
-        flip_pool = ctx.enter_context(tc.tile_pool(name="flip_pool", bufs=FLIP_RUN + 1))
-        q_pool = ctx.enter_context(tc.tile_pool(name="q_pool", bufs=3))
-        x_mx = ctx.enter_context(tc.tile_pool(name="x_mx", bufs=3))
-        q_mx = ctx.enter_context(tc.tile_pool(name="q_mx", bufs=SCORE_LAG + 2))
-        k_mx = ctx.enter_context(tc.tile_pool(name="k_mx", bufs=3))
+        grouped_pool = ctx.enter_context(tc.tile_pool(name="grouped_pool", bufs=3))
+        x_mx_pool = ctx.enter_context(tc.tile_pool(name="x_mx_pool", bufs=3))
+        k_mx_pool = ctx.enter_context(tc.tile_pool(name="k_mx_pool", bufs=3))
+        q_mx_pool = ctx.enter_context(tc.tile_pool(name="q_mx_pool", bufs=SCORE_LAG + 2))
         out_pool = ctx.enter_context(tc.tile_pool(name="out_pool", bufs=4))
         psum = ctx.enter_context(tc.psum_pool(name="psum", bufs=PSUM_BANKS))
 
-        def load_four_rows_a_partition(rows, tile_sb):
-            nc.sync.dma_start(out=tile_sb[:], in_=rows.rearrange("(p s) d -> p (s d)", s=PACK))
+        def mx_operand(pool, columns, label):
+            codes = pool.tile([P, columns], U32, name="%s_codes" % label, align_bytes=64)
+            scales = pool.tile([P, columns], U8, name="%s_scales" % label, align_bytes=64)
+            return codes, scales
+
+        def quantise(grouped, operand, columns):
+            codes, scales = operand
+            nc.vector.quantize_mx(
+                out=codes[:, columns].bitcast(FP8X4), scales=scales[:, columns], in_=grouped
+            )
+
+        def mx_pass(acc, stationary, stationary_columns, moving, moving_columns, start=True, stop=True):
+            nc.tensor.matmul_mx(
+                out=acc,
+                lhsT=stationary[0][:, stationary_columns].bitcast(FP8X4),
+                lhsT_scale=stationary[1][:, stationary_columns],
+                rhs=moving[0][:, moving_columns].bitcast(FP8X4),
+                rhs_scale=moving[1][:, moving_columns],
+                start=start,
+                stop=stop,
+            )
+
+        def sets(first, count=1):
+            return slice(first * SET, (first + count) * SET)
+
+        def load_four_rows_a_partition(rows, rows_sb):
+            nc.sync.dma_start(out=rows_sb[:], in_=rows.rearrange("(p s) d -> p (s d)", s=PACK))
 
         wq_sb = const.tile([P, PACK * D], BF16)
         wk_sb = const.tile([P, PACK * D], BF16)
@@ -72,166 +97,127 @@ def tile_siglipsdpaattention_pa_t_kernel(tc, x, Wq, bq, Wk, bk, out):
         make_identity(nc, ident[:])
 
         def features_to_partitions(rows_sb, grouped, copy_out):
-            words = rows_sb[:].bitcast(F32)
-            grouped_words = grouped[:].bitcast(F32).rearrange("p (c u) -> p c u", u=2)
-            for half in range(2):
-                flipped = psum.tile([P, 2, PAIR], F32, name="flipped", tag="bank")
-                for s in range(2):
-                    for u in range(2):
-                        first = (2 * half + s) * (D // 2) + u * P
-                        nc.tensor.transpose(
-                            flipped[:, u, s * P : (s + 1) * P], words[:, first : first + P], ident[:]
-                        )
+            pairs = rows_sb[:].bitcast(F32)
+            grouped_pairs = grouped[:].bitcast(F32).rearrange("p (c u) -> p c u", u=HALVES)
+            for bank in range(PACK // PER_BANK):
+                flipped = psum.tile([P, HALVES, PER_BANK * SET], F32, name="flipped", tag="bank")
+                for i in range(PER_BANK):
+                    s = PER_BANK * bank + i
+                    for u in range(HALVES):
+                        first = (s * HALVES + u) * P
+                        nc.tensor.transpose(flipped[:, u, sets(i)], pairs[:, first : first + P], ident[:])
                 copy_out(
-                    out=grouped_words[:, half * PAIR : (half + 1) * PAIR, :],
+                    out=grouped_pairs[:, sets(PER_BANK * bank, PER_BANK), :],
                     in_=flipped[:].rearrange("p u c -> p c u"),
                 )
 
-        def quantise(grouped_flat, codes, scales):
-            nc.vector.quantize_mx(out=codes.bitcast(FP8X4), scales=scales, in_=grouped_flat)
-
-        def mx_pass(acc, lhs, lhs_cols, rhs, rhs_cols, start, stop):
-            nc.tensor.matmul_mx(
-                out=acc,
-                lhsT=lhs[0][:, lhs_cols].bitcast(FP8X4),
-                lhsT_scale=lhs[1][:, lhs_cols],
-                rhs=rhs[0][:, rhs_cols].bitcast(FP8X4),
-                rhs_scale=rhs[1][:, rhs_cols],
-                start=start,
-                stop=stop,
-            )
-
-        def set_of(i):
-            return slice(i * P, (i + 1) * P)
-
-        weights = []
-        for label, w_sb in (("wq", wq_sb), ("wk", wk_sb)):
-            w_grouped = const.tile([P, PACK * D], BF16, name="%s_grouped" % label, align_bytes=64)
-            w_codes = const.tile([P, D], U32, name="%s_codes" % label, align_bytes=64)
-            w_scales = const.tile([P, D], U8, name="%s_scales" % label, align_bytes=64)
-            features_to_partitions(w_sb, w_grouped, nc.vector.tensor_copy)
-            weights.append((w_grouped, w_codes, w_scales))
-        for w_grouped, w_codes, w_scales in weights:
-            quantise(w_grouped[:], w_codes[:], w_scales[:])
-        wq_mx = (weights[0][1], weights[0][2])
-        wk_mx = (weights[1][1], weights[1][2])
+        wq_grouped = const.tile([P, PACK * D], BF16, align_bytes=64)
+        wk_grouped = const.tile([P, PACK * D], BF16, align_bytes=64)
+        features_to_partitions(wq_sb, wq_grouped, nc.vector.tensor_copy)
+        features_to_partitions(wk_sb, wk_grouped, nc.vector.tensor_copy)
+        wq_mx = mx_operand(const, D, "wq")
+        wk_mx = mx_operand(const, D, "wk")
+        quantise(wq_grouped[:], wq_mx, sets(0, PACK))
+        quantise(wk_grouped[:], wk_mx, sets(0, PACK))
 
         bq_f32 = const.tile([P, PACK], F32)
         bk_f32 = const.tile([P, PACK], F32)
         nc.vector.tensor_copy(out=bq_f32[:], in_=bq_bf[:])
         nc.vector.tensor_copy(out=bk_f32[:], in_=bk_bf[:])
-        bq_every_column = bq_f32[:].unsqueeze(1).to_broadcast([P, P, PACK])
-        bk_every_column = bk_f32[:].unsqueeze(1).to_broadcast([P, P, PACK])
+        bq_every_column = bq_f32[:].unsqueeze(1).to_broadcast([P, SET, PACK])
+        bk_every_column = bk_f32[:].unsqueeze(1).to_broadcast([P, SET, PACK])
 
-        x_codes = {}
-        q_codes = {}
-        k_codes = {}
-
-        x_grouped = {}
-
-        def flip_x(n):
-            x_grouped[n] = flip_pool.tile([P, PACK * BLOCK], BF16, name="x_grouped", align_bytes=64)
-            features_to_partitions(x_sb[n], x_grouped[n], nc.scalar.copy)
-
-        def quantise_x(n):
-            codes = x_mx.tile([P, BLOCK], U32, name="x_code_words", align_bytes=64)
-            scales = x_mx.tile([P, BLOCK], U8, name="x_scale_bytes", align_bytes=64)
-            quantise(x_grouped[n][:], codes[:], scales[:])
-            x_codes[n] = (codes, scales)
-
-        def scores(n, pair):
-            acc = psum.tile([P, 2, KEYS], F32, name="score_acc", tag="bank")
-            for i in range(2):
-                mx_pass(
-                    acc[:, i, :], q_codes[n], set_of(2 * pair + i),
-                    k_codes[n // BLOCKS_PER_BATCH], slice(0, KEYS), True, True,
-                )
-            logits = out_pool.tile([P, 2, KEYS], F32, name="logits")
-            nc.scalar.activation(
-                out=logits[:], in_=acc[:], func=COPY, bias=math.log(WINDOW), scale=1.0 / math.sqrt(D)
-            )
-            block_rows = out_rows[n * BLOCK : (n + 1) * BLOCK, :].rearrange("(m r) k -> m r k", r=WINDOW)
-            nc.sync.dma_start(out=block_rows[:, 2 * pair : 2 * pair + 2, :], in_=logits[:])
-
+        x_mx = {}
         q_grouped = {}
+        q_mx = {}
+        k_grouped = {}
+        k_mx = {}
 
-        def q_for_scalar(n):
-            q_grouped[n] = q_pool.tile([P, BLOCK, PACK], BF16, name="q_grouped", align_bytes=64)
-            q_planes = work.tile([P, PACK, PAIR], BF16, name="q_planes")
-            for jj in range(2):
-                qs_acc = psum.tile([P, 2, PAIR], F32, name="qs_acc", tag="bank")
-                for i in range(2):
-                    mx_pass(qs_acc[:, i, :], wq_mx, set_of(2 * jj + i), x_codes[n], slice(PAIR, 2 * PAIR), True, True)
-                for i in range(2):
-                    j = 2 * jj + i
+        def prepare_x(n):
+            x_grouped = grouped_pool.tile([P, PACK * BLOCK], BF16, name="x_grouped", align_bytes=64)
+            features_to_partitions(x_sb[n], x_grouped, nc.scalar.copy)
+            x_mx[n] = mx_operand(x_mx_pool, BLOCK, "x")
+            quantise(x_grouped[:], x_mx[n], sets(0, WINDOW))
+
+        def q_of_sets_2_and_3(n):
+            q_grouped[n] = grouped_pool.tile([P, BLOCK, PACK], BF16, name="q_grouped", align_bytes=64)
+            q_planes = grouped_pool.tile([P, PACK, 2 * SET], BF16, name="q_planes")
+            for bank in range(PACK // PER_BANK):
+                q_acc = psum.tile([P, PER_BANK, 2 * SET], F32, name="q_acc_planes", tag="bank")
+                for i in range(PER_BANK):
+                    mx_pass(q_acc[:, i, :], wq_mx, sets(PER_BANK * bank + i), x_mx[n], sets(2, 2))
+                for i in range(PER_BANK):
+                    j = PER_BANK * bank + i
                     nc.scalar.activation(
-                        out=q_planes[:, j, :], in_=qs_acc[:, i, :], func=IDENTITY,
+                        out=q_planes[:, j, :], in_=q_acc[:, i, :], func=IDENTITY,
                         bias=bq_f32[:, j : j + 1], scale=1.0,
                     )
             nc.gpsimd.tensor_scalar(
-                out=q_grouped[n][:, PAIR : 2 * PAIR, :], in0=q_planes[:].rearrange("p j c -> p c j"),
+                out=q_grouped[n][:, sets(2, 2), :], in0=q_planes[:].rearrange("p j c -> p c j"),
                 scalar1=1.0, scalar2=0.0, op0=MULT, op1=ADD,
             )
 
-        def q_for_vector(n):
+        def q_of_sets_0_and_1(n):
             for r in range(2):
-                qv_acc = psum.tile([P, PACK, P], F32, name="qv_acc", tag="bank")
+                q_acc = psum.tile([P, PACK, SET], F32, name="q_acc", tag="bank")
                 for j in range(PACK):
-                    mx_pass(qv_acc[:, j, :], wq_mx, set_of(j), x_codes[n], set_of(r), True, True)
+                    mx_pass(q_acc[:, j, :], wq_mx, sets(j), x_mx[n], sets(r))
                 nc.vector.tensor_tensor(
-                    out=q_grouped[n][:, set_of(r), :], in0=qv_acc[:].rearrange("p j c -> p c j"),
+                    out=q_grouped[n][:, sets(r), :], in0=q_acc[:].rearrange("p j c -> p c j"),
                     in1=bq_every_column, op=ADD,
                 )
 
         def quantise_q(n):
-            q_words = q_mx.tile([P, BLOCK], U32, name="q_words", align_bytes=64)
-            q_bytes = q_mx.tile([P, BLOCK], U8, name="q_bytes", align_bytes=64)
-            quantise(q_grouped[n][:].rearrange("p c j -> p (c j)"), q_words[:], q_bytes[:])
-            q_codes[n] = (q_words, q_bytes)
-
-        k_grouped = {}
+            q_mx[n] = mx_operand(q_mx_pool, BLOCK, "q")
+            quantise(q_grouped[n][:].rearrange("p c j -> p (c j)"), q_mx[n], sets(0, WINDOW))
 
         def merged_k(n):
-            k_acc = psum.tile([P, PACK, P], F32, name="k_acc", tag="bank")
+            k_acc = psum.tile([P, PACK, SET], F32, name="k_acc", tag="bank")
             for j in range(PACK):
                 for r in range(WINDOW):
-                    mx_pass(k_acc[:, j, :], wk_mx, set_of(j), x_codes[n], set_of(r), r == 0, r == WINDOW - 1)
-            k_grouped[n] = work.tile([P, P, PACK], BF16, name="k_grouped", align_bytes=64)
+                    mx_pass(
+                        k_acc[:, j, :], wk_mx, sets(j), x_mx[n], sets(r),
+                        start=(r == 0), stop=(r == WINDOW - 1),
+                    )
+            k_grouped[n] = grouped_pool.tile([P, SET, PACK], BF16, name="k_grouped", align_bytes=64)
             nc.vector.scalar_tensor_tensor(
                 out=k_grouped[n][:], in0=k_acc[:].rearrange("p j m -> p m j"), scalar=1.0 / WINDOW,
                 in1=bk_every_column, op0=MULT, op1=ADD,
             )
 
         def quantise_k(n):
-            b = n // BLOCKS_PER_BATCH
-            half = n % BLOCKS_PER_BATCH
-            if half == 0:
-                k_words = k_mx.tile([P, KEYS], U32, name="k_words", align_bytes=64)
-                k_bytes = k_mx.tile([P, KEYS], U8, name="k_bytes", align_bytes=64)
-                k_codes[b] = (k_words, k_bytes)
-            quantise(
-                k_grouped[n][:].rearrange("p m j -> p (m j)"),
-                k_codes[b][0][:, set_of(half)], k_codes[b][1][:, set_of(half)],
-            )
+            b, part = divmod(n, BLOCKS_PER_BATCH)
+            if part == 0:
+                k_mx[b] = mx_operand(k_mx_pool, KEYS, "k")
+            quantise(k_grouped[n][:].rearrange("p m j -> p (m j)"), k_mx[b], sets(part))
 
-        for m in range(FLIP_RUN):
-            flip_x(m)
-        quantise_x(0)
+        def scores(n):
+            block_rows = out_rows[n * BLOCK : (n + 1) * BLOCK, :].rearrange("(m r) k -> m r k", r=WINDOW)
+            keys_mx = k_mx[n // BLOCKS_PER_BATCH]
+            for bank in range(WINDOW // PER_BANK):
+                score_acc = psum.tile([P, PER_BANK, KEYS], F32, name="score_acc", tag="bank")
+                for i in range(PER_BANK):
+                    mx_pass(score_acc[:, i, :], q_mx[n], sets(PER_BANK * bank + i), keys_mx, sets(0, 2))
+                logits = out_pool.tile([P, PER_BANK, KEYS], F32, name="logits")
+                nc.scalar.activation(
+                    out=logits[:], in_=score_acc[:], func=COPY,
+                    bias=math.log(WINDOW), scale=1.0 / math.sqrt(D),
+                )
+                nc.sync.dma_start(
+                    out=block_rows[:, PER_BANK * bank : PER_BANK * (bank + 1), :], in_=logits[:]
+                )
+
+        prepare_x(0)
         for n in range(BLOCKS + SCORE_LAG):
-            if (n + 1) % FLIP_RUN == 0:
-                for m in range(n + 1, min(n + 1 + FLIP_RUN, BLOCKS)):
-                    flip_x(m)
             if n + 1 < BLOCKS:
-                quantise_x(n + 1)
+                prepare_x(n + 1)
             if 1 <= n <= BLOCKS:
                 quantise_q(n - 1)
-            if n >= SCORE_LAG:
-                scores(n - SCORE_LAG, 0)
             if n < BLOCKS:
-                q_for_scalar(n)
+                q_of_sets_2_and_3(n)
                 merged_k(n)
             if n >= SCORE_LAG:
-                scores(n - SCORE_LAG, 1)
+                scores(n - SCORE_LAG)
             if n < BLOCKS:
-                q_for_vector(n)
+                q_of_sets_0_and_1(n)
                 quantise_k(n)

import math
from contextlib import ExitStack

import concourse.mybir as mybir
from concourse.masks import make_identity

F32 = mybir.dt.float32
BF16 = mybir.dt.bfloat16
U32 = mybir.dt.uint32
U8 = mybir.dt.uint8
FP8X4 = mybir.dt.float8_e4m3fn_x4
ADD = mybir.AluOpType.add
MULT = mybir.AluOpType.mult
IDENTITY = mybir.ActivationFunctionType.Identity
COPY = mybir.ActivationFunctionType.Copy

P = 128
PACK = 4
D = P * PACK
BATCH = 8
TOKENS = 1024
WINDOW = 4
KEYS = TOKENS // WINDOW
SET = 128
BLOCK = SET * WINDOW
BLOCKS = BATCH * TOKENS // BLOCK
BLOCKS_PER_BATCH = TOKENS // BLOCK
PSUM_BANKS = 8
PER_BANK = 2
HALVES = 2
SCORE_LAG = 2

FLOPS = 2 * BATCH * TOKENS * D * D * 2 + 2 * BATCH * TOKENS * KEYS * D


def tile_siglipsdpaattention_pa_t_kernel(tc, x, Wq, bq, Wk, bk, out):
    nc = tc.nc
    x_rows = x.flatten_outer_dims()
    out_rows = out.flatten_outer_dims()

    with ExitStack() as ctx:
        ctx.enter_context(tc.manual_schedule())

        const = ctx.enter_context(tc.tile_pool(name="const", bufs=1))
        x_pool = ctx.enter_context(tc.tile_pool(name="x_pool", bufs=BLOCKS))
        grouped_pool = ctx.enter_context(tc.tile_pool(name="grouped_pool", bufs=3))
        x_mx_pool = ctx.enter_context(tc.tile_pool(name="x_mx_pool", bufs=3))
        k_mx_pool = ctx.enter_context(tc.tile_pool(name="k_mx_pool", bufs=3))
        q_mx_pool = ctx.enter_context(tc.tile_pool(name="q_mx_pool", bufs=SCORE_LAG + 2))
        out_pool = ctx.enter_context(tc.tile_pool(name="out_pool", bufs=4))
        psum = ctx.enter_context(tc.psum_pool(name="psum", bufs=PSUM_BANKS))

        def mx_operand(pool, columns, label):
            codes = pool.tile([P, columns], U32, name="%s_codes" % label, align_bytes=64)
            scales = pool.tile([P, columns], U8, name="%s_scales" % label, align_bytes=64)
            return codes, scales

        def quantise(grouped, operand, columns):
            codes, scales = operand
            nc.vector.quantize_mx(
                out=codes[:, columns].bitcast(FP8X4), scales=scales[:, columns], in_=grouped
            )

        def mx_pass(acc, stationary, stationary_columns, moving, moving_columns, start=True, stop=True):
            nc.tensor.matmul_mx(
                out=acc,
                lhsT=stationary[0][:, stationary_columns].bitcast(FP8X4),
                lhsT_scale=stationary[1][:, stationary_columns],
                rhs=moving[0][:, moving_columns].bitcast(FP8X4),
                rhs_scale=moving[1][:, moving_columns],
                start=start,
                stop=stop,
            )

        def sets(first, count=1):
            return slice(first * SET, (first + count) * SET)

        def load_four_rows_a_partition(rows, rows_sb):
            nc.sync.dma_start(out=rows_sb[:], in_=rows.rearrange("(p s) d -> p (s d)", s=PACK))

        wq_sb = const.tile([P, PACK * D], BF16)
        wk_sb = const.tile([P, PACK * D], BF16)
        load_four_rows_a_partition(Wq, wq_sb)
        load_four_rows_a_partition(Wk, wk_sb)
        x_sb = []
        for n in range(BLOCKS):
            x_block = x_pool.tile([P, PACK * D], BF16, name="x_block")
            load_four_rows_a_partition(x_rows[n * BLOCK : (n + 1) * BLOCK, :], x_block)
            x_sb.append(x_block)

        bq_bf = const.tile([P, PACK], BF16)
        bk_bf = const.tile([P, PACK], BF16)
        nc.scalar.dma_start(out=bq_bf[:], in_=bq.rearrange("(p j) -> p j", j=PACK))
        nc.scalar.dma_start(out=bk_bf[:], in_=bk.rearrange("(p j) -> p j", j=PACK))

        ident = const.tile([P, P], F32)
        make_identity(nc, ident[:])

        def features_to_partitions(rows_sb, grouped, copy_out):
            pairs = rows_sb[:].bitcast(F32)
            grouped_pairs = grouped[:].bitcast(F32).rearrange("p (c u) -> p c u", u=HALVES)
            for bank in range(PACK // PER_BANK):
                flipped = psum.tile([P, HALVES, PER_BANK * SET], F32, name="flipped", tag="bank")
                for i in range(PER_BANK):
                    s = PER_BANK * bank + i
                    for u in range(HALVES):
                        first = (s * HALVES + u) * P
                        nc.tensor.transpose(flipped[:, u, sets(i)], pairs[:, first : first + P], ident[:])
                copy_out(
                    out=grouped_pairs[:, sets(PER_BANK * bank, PER_BANK), :],
                    in_=flipped[:].rearrange("p u c -> p c u"),
                )

        wq_grouped = const.tile([P, PACK * D], BF16, align_bytes=64)
        wk_grouped = const.tile([P, PACK * D], BF16, align_bytes=64)
        features_to_partitions(wq_sb, wq_grouped, nc.vector.tensor_copy)
        features_to_partitions(wk_sb, wk_grouped, nc.vector.tensor_copy)
        wq_mx = mx_operand(const, D, "wq")
        wk_mx = mx_operand(const, D, "wk")
        quantise(wq_grouped[:], wq_mx, sets(0, PACK))
        quantise(wk_grouped[:], wk_mx, sets(0, PACK))

        bq_f32 = const.tile([P, PACK], F32)
        bk_f32 = const.tile([P, PACK], F32)
        nc.vector.tensor_copy(out=bq_f32[:], in_=bq_bf[:])
        nc.vector.tensor_copy(out=bk_f32[:], in_=bk_bf[:])
        bq_every_column = bq_f32[:].unsqueeze(1).to_broadcast([P, SET, PACK])
        bk_every_column = bk_f32[:].unsqueeze(1).to_broadcast([P, SET, PACK])

        x_mx = {}
        q_grouped = {}
        q_mx = {}
        k_grouped = {}
        k_mx = {}

        def prepare_x(n):
            x_grouped = grouped_pool.tile([P, PACK * BLOCK], BF16, name="x_grouped", align_bytes=64)
            features_to_partitions(x_sb[n], x_grouped, nc.scalar.copy)
            x_mx[n] = mx_operand(x_mx_pool, BLOCK, "x")
            quantise(x_grouped[:], x_mx[n], sets(0, WINDOW))

        def q_of_sets_2_and_3(n):
            q_grouped[n] = grouped_pool.tile([P, BLOCK, PACK], BF16, name="q_grouped", align_bytes=64)
            q_planes = grouped_pool.tile([P, PACK, 2 * SET], BF16, name="q_planes")
            for bank in range(PACK // PER_BANK):
                q_acc = psum.tile([P, PER_BANK, 2 * SET], F32, name="q_acc_planes", tag="bank")
                for i in range(PER_BANK):
                    mx_pass(q_acc[:, i, :], wq_mx, sets(PER_BANK * bank + i), x_mx[n], sets(2, 2))
                for i in range(PER_BANK):
                    j = PER_BANK * bank + i
                    nc.scalar.activation(
                        out=q_planes[:, j, :], in_=q_acc[:, i, :], func=IDENTITY,
                        bias=bq_f32[:, j : j + 1], scale=1.0,
                    )
            nc.gpsimd.tensor_scalar(
                out=q_grouped[n][:, sets(2, 2), :], in0=q_planes[:].rearrange("p j c -> p c j"),
                scalar1=1.0, scalar2=0.0, op0=MULT, op1=ADD,
            )

        def q_of_sets_0_and_1(n):
            for r in range(2):
                q_acc = psum.tile([P, PACK, SET], F32, name="q_acc", tag="bank")
                for j in range(PACK):
                    mx_pass(q_acc[:, j, :], wq_mx, sets(j), x_mx[n], sets(r))
                nc.vector.tensor_tensor(
                    out=q_grouped[n][:, sets(r), :], in0=q_acc[:].rearrange("p j c -> p c j"),
                    in1=bq_every_column, op=ADD,
                )

        def quantise_q(n):
            q_mx[n] = mx_operand(q_mx_pool, BLOCK, "q")
            quantise(q_grouped[n][:].rearrange("p c j -> p (c j)"), q_mx[n], sets(0, WINDOW))

        def merged_k(n):
            k_acc = psum.tile([P, PACK, SET], F32, name="k_acc", tag="bank")
            for j in range(PACK):
                for r in range(WINDOW):
                    mx_pass(
                        k_acc[:, j, :], wk_mx, sets(j), x_mx[n], sets(r),
                        start=(r == 0), stop=(r == WINDOW - 1),
                    )
            k_grouped[n] = grouped_pool.tile([P, SET, PACK], BF16, name="k_grouped", align_bytes=64)
            nc.vector.scalar_tensor_tensor(
                out=k_grouped[n][:], in0=k_acc[:].rearrange("p j m -> p m j"), scalar=1.0 / WINDOW,
                in1=bk_every_column, op0=MULT, op1=ADD,
            )

        def quantise_k(n):
            b, part = divmod(n, BLOCKS_PER_BATCH)
            if part == 0:
                k_mx[b] = mx_operand(k_mx_pool, KEYS, "k")
            quantise(k_grouped[n][:].rearrange("p m j -> p (m j)"), k_mx[b], sets(part))

        def scores(n):
            block_rows = out_rows[n * BLOCK : (n + 1) * BLOCK, :].rearrange("(m r) k -> m r k", r=WINDOW)
            keys_mx = k_mx[n // BLOCKS_PER_BATCH]
            for bank in range(WINDOW // PER_BANK):
                score_acc = psum.tile([P, PER_BANK, KEYS], F32, name="score_acc", tag="bank")
                for i in range(PER_BANK):
                    mx_pass(score_acc[:, i, :], q_mx[n], sets(PER_BANK * bank + i), keys_mx, sets(0, 2))
                logits = out_pool.tile([P, PER_BANK, KEYS], F32, name="logits")
                nc.scalar.activation(
                    out=logits[:], in_=score_acc[:], func=COPY,
                    bias=math.log(WINDOW), scale=1.0 / math.sqrt(D),
                )
                nc.sync.dma_start(
                    out=block_rows[:, PER_BANK * bank : PER_BANK * (bank + 1), :], in_=logits[:]
                )

        prepare_x(0)
        for n in range(BLOCKS + SCORE_LAG):
            if n + 1 < BLOCKS:
                prepare_x(n + 1)
            if 1 <= n <= BLOCKS:
                quantise_q(n - 1)
            if n < BLOCKS:
                q_of_sets_2_and_3(n)
                merged_k(n)
            if n >= SCORE_LAG:
                scores(n - SCORE_LAG)
            if n < BLOCKS:
                q_of_sets_0_and_1(n)
                quantise_k(n)
